import numpy as np
import ml_dtypes


def mxq(x, axis, fmt="e4m3"):
    dtype, down = {"e4m3": (ml_dtypes.float8_e4m3fn, 7), "e5m2": (ml_dtypes.float8_e5m2, 14)}[fmt]
    v = np.moveaxis(np.asarray(x, np.float32).astype(ml_dtypes.bfloat16).astype(np.float64), axis, -1)
    blocks = v.reshape(v.shape[:-1] + (-1, 32))
    amax = np.abs(blocks).max(-1, keepdims=True)
    byte = np.maximum(np.where(amax > 0, np.frexp(amax)[1] - 1 + 127, 0) - down, 1)
    scale = np.exp2(byte - 127.0)
    codes = (blocks / scale).astype(np.float32).astype(dtype).astype(np.float64)
    return np.moveaxis((codes * scale).reshape(v.shape), -1, axis)


WIDE = False


def mx_kscale(k):
    if not WIDE:
        return np.ones(k)
    levels = np.array([10, -10, 5, -5, 0])
    a = np.random.permutation(np.resize(levels, k // 512 * 4)).reshape(k // 512, 4)
    idx = np.arange(k)
    return np.exp2(a[idx // 512, idx % 128 // 32])


BF16 = ml_dtypes.bfloat16


def bf(x):
    return np.asarray(x, np.float32).astype(BF16)


def f64(x):
    return np.asarray(x).astype(np.float64)


NA, NB, ND, ED = 64, 64, 1024, 512
K1 = 2 * ED


def setup_inputs():
    s, t = mx_kscale(K1), mx_kscale(ED)
    return {"edge_embeds": bf(np.random.standard_normal((NA, NB, K1)) * s),
            "a_proj": bf(np.random.standard_normal((NA, ED)) * 0.5 * t),
            "b_proj": bf(np.random.standard_normal((NB, ED)) * 0.5 * t),
            "We": bf(np.random.standard_normal((K1, ED)) * 0.7 / np.sqrt(K1) / s[:, None] * t),
            "be1": bf(np.random.standard_normal(ED) * 0.3 * t),
            "We2": bf(np.random.standard_normal((ED, ED)) * 0.5 / np.sqrt(ED) / t[:, None]),
            "be2": bf(np.random.standard_normal(ED) * 0.1)}


def reference(edge_embeds, a_proj, b_proj, We, be1, We2, be2):
    h = f64(a_proj)[:, None, :] + f64(b_proj)[None, :, :] + (mxq(f64(edge_embeds), 2, "e4m3") @ mxq(f64(We), 0, "e4m3")) + f64(be1)
    h = np.maximum(h, 0.0)
    edge_latent = np.maximum((mxq(h, 2, "e4m3") @ mxq(f64(We2), 0, "e4m3")) + f64(be2), 0.0)
    sum_a = edge_latent.sum(axis=1)
    sum_b = edge_latent.sum(axis=0)
    return edge_latent, sum_a, sum_b

@@ -1,0 +1,292 @@
+from contextlib import ExitStack
+
+import concourse.mybir as mybir
+from concourse.masks import make_identity
+
+F32 = mybir.dt.float32
+BF16 = mybir.dt.bfloat16
+U32 = mybir.dt.uint32
+U8 = mybir.dt.uint8
+FP8X4 = mybir.dt.float8_e4m3fn_x4
+ADD = mybir.AluOpType.add
+RELU = mybir.ActivationFunctionType.Relu
+
+P = 128
+NA = 64
+NB = 64
+K1 = 1024
+ED = 512
+CH = 512
+NCH = NA * NB // CH
+FLOPS = 2 * NA * NB * K1 * ED + 2 * NA * NB * ED * ED
+
+MANUAL = True
+H_ON_VECTOR = (True, False, True, False)
+
+
+def tile_bipartiteneuralmessagepassinglayer_pa_t_kernel(
+    tc, edge_embeds, a_proj, b_proj, We, be1, We2, be2, out_0, out_1, out_2
+):
+    nc = tc.nc
+    x_rows = edge_embeds.rearrange("i j k -> (i j) k")
+    o_rows = out_0.rearrange("i j f -> (i j) f")
+
+    with ExitStack() as ctx:
+        const = ctx.enter_context(tc.tile_pool(name="const", bufs=1))
+        work = ctx.enter_context(tc.tile_pool(name="work", bufs=2))
+        psum = ctx.enter_context(tc.psum_pool(name="psum", bufs=8))
+        if MANUAL:
+            ctx.enter_context(tc.manual_schedule())
+
+        def bank(label):
+            return psum.tile([P, 512], F32, tag="bank", name=label)
+
+        ident = const.tile([P, P], F32, name="ident")
+        make_identity(nc, ident[:])
+        ab_bf = const.tile([P, ED], BF16, name="ab_bf")
+        bias_bf = const.tile([P, P], BF16, name="bias_bf")
+        st = const.tile([P, 4, P], F32, name="st")
+        nc.vector.memset(bias_bf[:], 0.0)
+        nc.vector.memset(st[:], 0.0)
+        nc.scalar.dma_start(out=ab_bf[0:NA, :], in_=a_proj)
+        nc.scalar.dma_start(out=ab_bf[NA:P, :], in_=b_proj)
+        nc.scalar.dma_start(out=bias_bf[0:4, :], in_=be1.rearrange("(m f) -> m f", m=4))
+        nc.scalar.dma_start(out=bias_bf[4:8, :], in_=be2.rearrange("(m f) -> m f", m=4))
+
+        xs = []
+        for c in range(NCH):
+            xs.append(const.tile([P, 4, K1], BF16, name="x%d" % c))
+        wraw = const.tile([P, 4, 2 * ED], BF16, name="wraw")
+        w2raw = const.tile([P, 4, ED], BF16, name="w2raw")
+        we_view = We.rearrange("(gu p e) c -> p gu (e c)", gu=4, p=P, e=2)
+
+        def load_x(c, t0, t1):
+            rows = x_rows[c * CH + t0 * P : c * CH + t1 * P, :]
+            nc.sync.dma_start(out=xs[c][:, t0:t1, :], in_=rows.rearrange("(t p) k -> p t k", p=P))
+
+        load_x(0, 0, 2)
+        load_x(0, 2, 4)
+        nc.sync.dma_start(out=wraw[:, 0:2, :], in_=we_view[:, 0:2, :])
+        nc.sync.dma_start(out=wraw[:, 2:4, :], in_=we_view[:, 2:4, :])
+        load_x(1, 0, 4)
+        nc.sync.dma_start(out=w2raw[:], in_=We2.rearrange("(t p) c -> p t c", p=P))
+        for c in range(2, NCH):
+            load_x(c, 0, 4)
+
+        ab32 = const.tile([P, ED], F32, name="ab32")
+        bias32 = const.tile([P, P], F32, name="bias32")
+        nc.vector.tensor_copy(out=ab32[:], in_=ab_bf[:])
+        nc.vector.tensor_copy(out=bias32[:], in_=bias_bf[:])
+        ps_ab = bank("ps_ab")
+        for m in range(4):
+            nc.tensor.transpose(ps_ab[:, m * P : (m + 1) * P], ab32[:, m * P : (m + 1) * P], ident[:])
+        ps_bias = bank("ps_bias")
+        nc.tensor.transpose(ps_bias[:, 0:P], bias32[:], ident[:])
+        biasT = const.tile([P, 8], F32, name="biasT")
+        abT = const.tile([P, 4, P], F32, name="abT")
+        nc.vector.tensor_copy(out=biasT[:], in_=ps_bias[:, 0:8])
+        nc.vector.tensor_copy(
+            out=abT[:, :, 0:NA], in_=ps_ab[:].rearrange("p (m r) -> p m r", m=4)[:, :, 0:NA]
+        )
+        for m in range(4):
+            nc.vector.tensor_scalar_add(
+                out=abT[:, m, NA:P], in0=ps_ab[:, m * P + NA : (m + 1) * P], scalar1=biasT[:, m : m + 1]
+            )
+
+        wg = const.tile([P, 2, ED, 4], BF16, name="wg", align_bytes=64)
+        wq = const.tile([P, 2 * ED], U32, name="wq", align_bytes=64)
+        wsc = const.tile([P, 2 * ED], U8, name="wsc", align_bytes=64)
+        w2g = const.tile([P, ED, 4], BF16, name="w2g", align_bytes=64)
+        w2q = const.tile([P, ED], U32, name="w2q", align_bytes=64)
+        w2sc = const.tile([P, ED], U8, name="w2sc", align_bytes=64)
+
+        def regroup(eng_copy, dst, src):
+            eng_copy(
+                out=dst.rearrange("p (c i) t -> p c t i", i=4),
+                in_=src.rearrange("p t (c i) -> p c t i", i=4),
+            )
+
+        def prep_we():
+            for g in range(2):
+                src = wraw[:, 2 * g : 2 * g + 2, :].rearrange("p u (e c) -> p (u e) c", e=2)
+                regroup(nc.vector.tensor_copy, wg[:, g, :, :], src)
+            nc.vector.quantize_mx(
+                out=wq[:].bitcast(FP8X4),
+                scales=wsc[:],
+                in_=wg[:].rearrange("p g c t -> p (g c t)"),
+            )
+
+        def prep_we2_regroup():
+            regroup(nc.scalar.copy, w2g[:], w2raw[:])
+
+        def prep_we2_quant():
+            nc.vector.quantize_mx(
+                out=w2q[:].bitcast(FP8X4), scales=w2sc[:], in_=w2g[:].rearrange("p c t -> p (c t)")
+            )
+
+        xg = {}
+        xq = {}
+        xsc = {}
+        yy = {}
+        hg = {}
+        hq = {}
+        hsc = {}
+        lt = {}
+        lo = {}
+
+        def xt_bank(c, b):
+            g = b // 2
+            eh = b % 2
+            if b == 0:
+                xg[c] = work.tile([P, 2, CH, 2], F32, name="xg%d" % c, tag="xg", align_bytes=64)
+            pb = bank("xt%d_%d" % (c, b))
+            for u in range(2):
+                for tl in range(2):
+                    words = xs[c][:, 2 * eh + tl, :].bitcast(F32)
+                    nc.tensor.transpose(
+                        pb[:, u * 256 + tl * P : u * 256 + (tl + 1) * P],
+                        words[:, 256 * g + P * u : 256 * g + P * (u + 1)],
+                        ident[:],
+                    )
+            nc.scalar.copy(
+                out=xg[c][:, g, eh * 256 : (eh + 1) * 256, :],
+                in_=pb[:].rearrange("p (u e) -> p e u", u=2),
+            )
+
+        def quant_x(c):
+            xq[c] = work.tile([P, 2 * CH], U32, name="xq%d" % c, tag="xq", align_bytes=64)
+            xsc[c] = work.tile([P, 2 * CH], U8, name="xsc%d" % c, tag="xsc", align_bytes=64)
+            nc.vector.quantize_mx(
+                out=xq[c][:].bitcast(FP8X4),
+                scales=xsc[c][:],
+                in_=xg[c][:].rearrange("p g e u -> p (g e u)").bitcast(BF16),
+            )
+
+        def stage1(c, m):
+            if m == 0:
+                yy[c] = work.tile([P, 4, CH], BF16, name="y%d" % c, tag="y")
+            pb = bank("p1_%d_%d" % (c, m))
+            for g in range(2):
+                cols = slice(g * ED + m * P, g * ED + (m + 1) * P)
+                nc.tensor.matmul_mx(
+                    out=pb[:],
+                    lhsT=wq[:, cols].bitcast(FP8X4),
+                    lhsT_scale=wsc[:, cols],
+                    rhs=xq[c][:, g * CH : (g + 1) * CH].bitcast(FP8X4),
+                    rhs_scale=xsc[c][:, g * CH : (g + 1) * CH],
+                    start=(g == 0),
+                    stop=(g == 1),
+                )
+            for il in range(8):
+                i = 8 * c + il
+                nc.vector.scalar_tensor_tensor(
+                    out=yy[c][:, m, il * NB : (il + 1) * NB],
+                    in0=pb[:, il * NB : (il + 1) * NB],
+                    scalar=abT[:, m, i : i + 1],
+                    in1=abT[:, m, NA:P],
+                    op0=ADD,
+                    op1=ADD,
+                )
+
+        def relu_regroup(c):
+            hg[c] = work.tile([P, CH, 4], BF16, name="hg%d" % c, tag="hg", align_bytes=64)
+            nc.vector.tensor_scalar_max(
+                out=hg[c][:].rearrange("p (c i) t -> p c t i", i=4),
+                in0=yy[c][:].rearrange("p t (c i) -> p c t i", i=4),
+                scalar1=0.0,
+            )
+
+        def quant_h(c):
+            hq[c] = work.tile([P, CH], U32, name="hq%d" % c, tag="hq", align_bytes=64)
+            hsc[c] = work.tile([P, CH], U8, name="hsc%d" % c, tag="hsc", align_bytes=64)
+            nc.vector.quantize_mx(
+                out=hq[c][:].bitcast(FP8X4),
+                scales=hsc[c][:],
+                in_=hg[c][:].rearrange("p e t -> p (e t)"),
+            )
+
+        def stage2(c, m):
+            if m == 0:
+                lt[c] = work.tile([P, 4, CH], F32, name="lt%d" % c, tag="lt", bufs=3)
+            pb = bank("p2_%d_%d" % (c, m))
+            cols = slice(m * P, (m + 1) * P)
+            nc.tensor.matmul_mx(
+                out=pb[:],
+                lhsT=w2q[:, cols].bitcast(FP8X4),
+                lhsT_scale=w2sc[:, cols],
+                rhs=hq[c][:].bitcast(FP8X4),
+                rhs_scale=hsc[c][:],
+                start=True,
+                stop=True,
+            )
+            for il in range(8):
+                i = 8 * c + il
+                nc.scalar.activation(
+                    out=lt[c][:, m, il * NB : (il + 1) * NB],
+                    in_=pb[:, il * NB : (il + 1) * NB],
+                    func=RELU,
+                    bias=biasT[:, 4 + m : 5 + m],
+                    scale=1.0,
+                    accum_out=st[:, m, i : i + 1],
+                )
+
+        def sum_b(c):
+            s1 = work.tile([P, 4, 256], F32, name="s1_%d" % c, tag="s1", bufs=1)
+            s2 = work.tile([P, 4, P], F32, name="s2_%d" % c, tag="s2", bufs=1)
+            nc.gpsimd.tensor_tensor(out=s1[:], in0=lt[c][:, :, 0:256], in1=lt[c][:, :, 256:512], op=ADD)
+            nc.gpsimd.tensor_tensor(out=s2[:], in0=s1[:, :, 0:P], in1=s1[:, :, P:256], op=ADD)
+            nc.gpsimd.tensor_tensor(out=st[:, :, NA:P], in0=st[:, :, NA:P], in1=s2[:, :, 0:NB], op=ADD)
+            nc.gpsimd.tensor_tensor(out=st[:, :, NA:P], in0=st[:, :, NA:P], in1=s2[:, :, NB:P], op=ADD)
+
+        def back(c, tl):
+            if tl == 0:
+                lo[c] = work.tile([P, 4, ED], F32, name="lo%d" % c, tag="lo")
+            pb = bank("lb%d_%d" % (c, tl))
+            for m in range(4):
+                nc.tensor.transpose(
+                    pb[:, m * P : (m + 1) * P], lt[c][:, m, tl * P : (tl + 1) * P], ident[:]
+                )
+            if H_ON_VECTOR[tl]:
+                nc.vector.tensor_copy(out=lo[c][:, tl, :], in_=pb[:])
+            else:
+                nc.scalar.copy(out=lo[c][:, tl, :], in_=pb[:])
+
+        def store(c):
+            rows = o_rows[c * CH : (c + 1) * CH, :]
+            nc.sync.dma_start(out=rows.rearrange("(t p) f -> p t f", p=P), in_=lo[c][:])
+
+        for k in range(-1, NCH + 2):
+            for b in range(4):
+                if 0 <= k + 1 < NCH:
+                    xt_bank(k + 1, b)
+                if b == 0 and 0 <= k - 1 < NCH:
+                    relu_regroup(k - 1)
+                if 0 <= k - 2 < NCH:
+                    back(k - 2, b)
+                if b == 1 and 0 <= k - 1 < NCH:
+                    quant_h(k - 1)
+            if 0 <= k - 2 < NCH:
+                store(k - 2)
+            if k == -1:
+                prep_we()
+            if k == 0:
+                prep_we2_regroup()
+            for m in range(4):
+                if 0 <= k - 1 < NCH:
+                    stage2(k - 1, m)
+                if 0 <= k < NCH:
+                    stage1(k, m)
+                if m == 1 and 0 <= k + 1 < NCH:
+                    quant_x(k + 1)
+            if k == 0:
+                prep_we2_quant()
+            if 0 <= k - 1 < NCH:
+                sum_b(k - 1)
+
+        pb = bank("ps_sum")
+        for m in range(4):
+            nc.tensor.transpose(pb[:, m * P : (m + 1) * P], st[:, m, :], ident[:])
+        so = const.tile([P, ED], F32, name="so")
+        nc.vector.tensor_copy(out=so[:], in_=pb[:])
+        nc.sync.dma_start(out=out_1, in_=so[0:NA, :])
+        nc.sync.dma_start(out=out_2, in_=so[NA:P, :])

@@ -34,7 +34,8 @@ def tile_bipartiteneuralmessagepassinglayer_pa_t_kernel(
     with ExitStack() as ctx:
         const = ctx.enter_context(tc.tile_pool(name="const", bufs=1))
         work = ctx.enter_context(tc.tile_pool(name="work", bufs=2))
-        psum = ctx.enter_context(tc.psum_pool(name="psum", bufs=8))
+        psum = ctx.enter_context(tc.psum_pool(name="psum", bufs=7))
+        psacc = ctx.enter_context(tc.psum_pool(name="psacc", bufs=1))
         if MANUAL:
             ctx.enter_context(tc.manual_schedule())
 
@@ -43,6 +44,10 @@ def tile_bipartiteneuralmessagepassinglayer_pa_t_kernel(
 
         ident = const.tile([P, P], F32, name="ident")
         make_identity(nc, ident[:])
+        sel = const.tile([P, P], F32, name="sel")
+        nc.vector.tensor_tensor(out=sel[:, 0:NB], in0=ident[:, 0:NB], in1=ident[:, NB:P], op=ADD)
+        nc.vector.tensor_tensor(out=sel[:, NB:P], in0=ident[:, 0:NB], in1=ident[:, NB:P], op=ADD)
+        acc = psacc.tile([P, ED], F32, name="acc")
         ab_bf = const.tile([P, ED], BF16, name="ab_bf")
         bias_bf = const.tile([P, P], BF16, name="bias_bf")
         st = const.tile([P, 4, P], F32, name="st")
@@ -230,14 +235,6 @@ def tile_bipartiteneuralmessagepassinglayer_pa_t_kernel(
                     accum_out=st[:, m, i : i + 1],
                 )
 
-        def sum_b(c):
-            s1 = work.tile([P, 4, 256], F32, name="s1_%d" % c, tag="s1", bufs=1)
-            s2 = work.tile([P, 4, P], F32, name="s2_%d" % c, tag="s2", bufs=1)
-            nc.gpsimd.tensor_tensor(out=s1[:], in0=lt[c][:, :, 0:256], in1=lt[c][:, :, 256:512], op=ADD)
-            nc.gpsimd.tensor_tensor(out=s2[:], in0=s1[:, :, 0:P], in1=s1[:, :, P:256], op=ADD)
-            nc.gpsimd.tensor_tensor(out=st[:, :, NA:P], in0=st[:, :, NA:P], in1=s2[:, :, 0:NB], op=ADD)
-            nc.gpsimd.tensor_tensor(out=st[:, :, NA:P], in0=st[:, :, NA:P], in1=s2[:, :, NB:P], op=ADD)
-
         def back(c, tl):
             if tl == 0:
                 lo[c] = work.tile([P, 4, ED], F32, name="lo%d" % c, tag="lo")
@@ -245,6 +242,15 @@ def tile_bipartiteneuralmessagepassinglayer_pa_t_kernel(
             for m in range(4):
                 nc.tensor.transpose(
                     pb[:, m * P : (m + 1) * P], lt[c][:, m, tl * P : (tl + 1) * P], ident[:]
+                )
+            for m in range(4):
+                nc.tensor.matmul(
+                    out=acc[:, m * P : (m + 1) * P],
+                    lhsT=lt[c][:, m, tl * P : (tl + 1) * P],
+                    rhs=ident[:],
+                    is_transpose=True,
+                    start=(c == 0 and tl == 0 and m == 0),
+                    stop=(c == NCH - 1 and tl == 3 and m == 3),
                 )
             if H_ON_VECTOR[tl]:
                 nc.vector.tensor_copy(out=lo[c][:, tl, :], in_=pb[:])
@@ -280,13 +286,17 @@ def tile_bipartiteneuralmessagepassinglayer_pa_t_kernel(
                     quant_x(k + 1)
             if k == 0:
                 prep_we2_quant()
-            if 0 <= k - 1 < NCH:
-                sum_b(k - 1)
 
-        pb = bank("ps_sum")
+        pa = bank("ps_suma")
         for m in range(4):
-            nc.tensor.transpose(pb[:, m * P : (m + 1) * P], st[:, m, :], ident[:])
-        so = const.tile([P, ED], F32, name="so")
-        nc.vector.tensor_copy(out=so[:], in_=pb[:])
-        nc.sync.dma_start(out=out_1, in_=so[0:NA, :])
-        nc.sync.dma_start(out=out_2, in_=so[NA:P, :])
+            nc.tensor.transpose(pa[:, m * P : (m + 1) * P], st[:, m, :], ident[:])
+        so_a = const.tile([P, ED], F32, name="so_a")
+        nc.scalar.copy(out=so_a[:], in_=pa[:])
+        nc.sync.dma_start(out=out_1, in_=so_a[0:NA, :])
+        acc_sb = const.tile([P, ED], F32, name="acc_sb")
+        nc.vector.tensor_copy(out=acc_sb[:], in_=acc[:])
+        pb = bank("ps_sumb")
+        nc.tensor.matmul(out=pb[:], lhsT=sel[:], rhs=acc_sb[:], start=True, stop=True)
+        so_b = const.tile([P, ED], F32, name="so_b")
+        nc.vector.tensor_copy(out=so_b[:], in_=pb[:])
+        nc.sync.dma_start(out=out_2, in_=so_b[0:NB, :])

@@ -9,6 +9,9 @@ U32 = mybir.dt.uint32
 U8 = mybir.dt.uint8
 FP8X4 = mybir.dt.float8_e4m3fn_x4
 ADD = mybir.AluOpType.add
+MIN = mybir.AluOpType.min
+MAX = mybir.AluOpType.max
+AX_X = mybir.AxisListType.X
 RELU = mybir.ActivationFunctionType.Relu
 
 P = 128
@@ -21,7 +24,8 @@ NCH = NA * NB // CH
 FLOPS = 2 * NA * NB * K1 * ED + 2 * NA * NB * ED * ED
 
 MANUAL = True
-H_ON_VECTOR = (True, False, True, False)
+H_ON_VECTOR = (True, False, False, False)
+BF16_MAX = (2.0 - 2.0 ** -7) * 2.0 ** 127
 
 
 def tile_bipartiteneuralmessagepassinglayer_pa_t_kernel(
@@ -69,10 +73,10 @@ def tile_bipartiteneuralmessagepassinglayer_pa_t_kernel(
             rows = x_rows[c * CH + t0 * P : c * CH + t1 * P, :]
             nc.sync.dma_start(out=xs[c][:, t0:t1, :], in_=rows.rearrange("(t p) k -> p t k", p=P))
 
-        load_x(0, 0, 2)
-        load_x(0, 2, 4)
         nc.sync.dma_start(out=wraw[:, 0:2, :], in_=we_view[:, 0:2, :])
         nc.sync.dma_start(out=wraw[:, 2:4, :], in_=we_view[:, 2:4, :])
+        load_x(0, 0, 2)
+        load_x(0, 2, 4)
         load_x(1, 0, 4)
         nc.sync.dma_start(out=w2raw[:], in_=We2.rearrange("(t p) c -> p t c", p=P))
         for c in range(2, NCH):
@@ -153,7 +157,8 @@ def tile_bipartiteneuralmessagepassinglayer_pa_t_kernel(
                         words[:, 256 * g + P * u : 256 * g + P * (u + 1)],
                         ident[:],
                     )
-            nc.scalar.copy(
+            copy_out = nc.vector.tensor_copy if (c == 0 and g == 1) else nc.scalar.copy
+            copy_out(
                 out=xg[c][:, g, eh * 256 : (eh + 1) * 256, :],
                 in_=pb[:].rearrange("p (u e) -> p e u", u=2),
             )
@@ -195,10 +200,13 @@ def tile_bipartiteneuralmessagepassinglayer_pa_t_kernel(
 
         def relu_regroup(c):
             hg[c] = work.tile([P, CH, 4], BF16, name="hg%d" % c, tag="hg", align_bytes=64)
-            nc.vector.tensor_scalar_max(
-                out=hg[c][:].rearrange("p (c i) t -> p c t i", i=4),
-                in0=yy[c][:].rearrange("p t (c i) -> p c t i", i=4),
-                scalar1=0.0,
+            nc.gpsimd.tensor_scalar(
+                out=hg[c][:],
+                in0=yy[c][:].rearrange("p t e -> p e t"),
+                scalar1=BF16_MAX,
+                scalar2=0.0,
+                op0=MIN,
+                op1=MAX,
             )
 
         def quant_h(c):
@@ -224,16 +232,17 @@ def tile_bipartiteneuralmessagepassinglayer_pa_t_kernel(
                 start=True,
                 stop=True,
             )
-            for il in range(8):
-                i = 8 * c + il
-                nc.scalar.activation(
-                    out=lt[c][:, m, il * NB : (il + 1) * NB],
-                    in_=pb[:, il * NB : (il + 1) * NB],
-                    func=RELU,
-                    bias=biasT[:, 4 + m : 5 + m],
-                    scale=1.0,
-                    accum_out=st[:, m, i : i + 1],
-                )
+            nc.scalar.activation(
+                out=lt[c][:, m, :], in_=pb[:], func=RELU, bias=biasT[:, 4 + m : 5 + m], scale=1.0
+            )
+
+        def sum_a(c):
+            nc.vector.tensor_reduce(
+                out=st[:, :, 8 * c : 8 * c + 8],
+                in_=lt[c][:].rearrange("p m (i j) -> p m i j", j=NB),
+                axis=AX_X,
+                op=ADD,
+            )
 
         def back(c, tl):
             if tl == 0:
@@ -257,10 +266,11 @@ def tile_bipartiteneuralmessagepassinglayer_pa_t_kernel(
             else:
                 nc.scalar.copy(out=lo[c][:, tl, :], in_=pb[:])
 
-        def store(c):
-            rows = o_rows[c * CH : (c + 1) * CH, :]
-            nc.sync.dma_start(out=rows.rearrange("(t p) f -> p t f", p=P), in_=lo[c][:])
+        def store(c, t0, t1):
+            rows = o_rows[c * CH + t0 * P : c * CH + t1 * P, :]
+            nc.sync.dma_start(out=rows.rearrange("(t p) f -> p t f", p=P), in_=lo[c][:, t0:t1, :])
 
+        prep_we()
         for k in range(-1, NCH + 2):
             for b in range(4):
                 if 0 <= k + 1 < NCH:
@@ -269,21 +279,23 @@ def tile_bipartiteneuralmessagepassinglayer_pa_t_kernel(
                     relu_regroup(k - 1)
                 if 0 <= k - 2 < NCH:
                     back(k - 2, b)
+                    if k - 2 == NCH - 1:
+                        store(k - 2, b, b + 1)
+                    if b == 0:
+                        sum_a(k - 2)
                 if b == 1 and 0 <= k - 1 < NCH:
                     quant_h(k - 1)
-            if 0 <= k - 2 < NCH:
-                store(k - 2)
-            if k == -1:
-                prep_we()
+            if 0 <= k - 2 < NCH - 1:
+                store(k - 2, 0, 4)
             if k == 0:
                 prep_we2_regroup()
-            for m in range(4):
-                if 0 <= k - 1 < NCH:
-                    stage2(k - 1, m)
-                if 0 <= k < NCH:
-                    stage1(k, m)
-                if m == 1 and 0 <= k + 1 < NCH:
+            for step in range(5):
+                if step < 4 and 0 <= k < NCH:
+                    stage1(k, step)
+                if step == 1 and 0 <= k + 1 < NCH:
                     quant_x(k + 1)
+                if step > 0 and 0 <= k - 1 < NCH:
+                    stage2(k - 1, step - 1)
             if k == 0:
                 prep_we2_quant()
 

@@ -9,8 +9,6 @@ U32 = mybir.dt.uint32
 U8 = mybir.dt.uint8
 FP8X4 = mybir.dt.float8_e4m3fn_x4
 ADD = mybir.AluOpType.add
-MIN = mybir.AluOpType.min
-MAX = mybir.AluOpType.max
 AX_X = mybir.AxisListType.X
 RELU = mybir.ActivationFunctionType.Relu
 
@@ -24,8 +22,6 @@ NCH = NA * NB // CH
 FLOPS = 2 * NA * NB * K1 * ED + 2 * NA * NB * ED * ED
 
 MANUAL = True
-H_ON_VECTOR = (True, False, False, False)
-BF16_MAX = (2.0 - 2.0 ** -7) * 2.0 ** 127
 
 
 def tile_bipartiteneuralmessagepassinglayer_pa_t_kernel(
@@ -200,13 +196,10 @@ def tile_bipartiteneuralmessagepassinglayer_pa_t_kernel(
 
         def relu_regroup(c):
             hg[c] = work.tile([P, CH, 4], BF16, name="hg%d" % c, tag="hg", align_bytes=64)
-            nc.gpsimd.tensor_scalar(
-                out=hg[c][:],
-                in0=yy[c][:].rearrange("p t e -> p e t"),
-                scalar1=BF16_MAX,
-                scalar2=0.0,
-                op0=MIN,
-                op1=MAX,
+            nc.vector.tensor_scalar_max(
+                out=hg[c][:].rearrange("p (c i) t -> p c t i", i=4),
+                in0=yy[c][:].rearrange("p t (c i) -> p c t i", i=4),
+                scalar1=0.0,
             )
 
         def quant_h(c):
@@ -236,10 +229,11 @@ def tile_bipartiteneuralmessagepassinglayer_pa_t_kernel(
                 out=lt[c][:, m, :], in_=pb[:], func=RELU, bias=biasT[:, 4 + m : 5 + m], scale=1.0
             )
 
-        def sum_a(c):
+        def sum_a(c, half):
+            ms = slice(2 * half, 2 * half + 2)
             nc.vector.tensor_reduce(
-                out=st[:, :, 8 * c : 8 * c + 8],
-                in_=lt[c][:].rearrange("p m (i j) -> p m i j", j=NB),
+                out=st[:, ms, 8 * c : 8 * c + 8],
+                in_=lt[c][:, ms, :].rearrange("p m (i j) -> p m i j", j=NB),
                 axis=AX_X,
                 op=ADD,
             )
@@ -252,6 +246,9 @@ def tile_bipartiteneuralmessagepassinglayer_pa_t_kernel(
                 nc.tensor.transpose(
                     pb[:, m * P : (m + 1) * P], lt[c][:, m, tl * P : (tl + 1) * P], ident[:]
                 )
+            nc.scalar.copy(out=lo[c][:, tl, :], in_=pb[:])
+
+        def accumulate(c, tl):
             for m in range(4):
                 nc.tensor.matmul(
                     out=acc[:, m * P : (m + 1) * P],
@@ -261,43 +258,51 @@ def tile_bipartiteneuralmessagepassinglayer_pa_t_kernel(
                     start=(c == 0 and tl == 0 and m == 0),
                     stop=(c == NCH - 1 and tl == 3 and m == 3),
                 )
-            if H_ON_VECTOR[tl]:
-                nc.vector.tensor_copy(out=lo[c][:, tl, :], in_=pb[:])
-            else:
-                nc.scalar.copy(out=lo[c][:, tl, :], in_=pb[:])
 
         def store(c, t0, t1):
             rows = o_rows[c * CH + t0 * P : c * CH + t1 * P, :]
             nc.sync.dma_start(out=rows.rearrange("(t p) f -> p t f", p=P), in_=lo[c][:, t0:t1, :])
 
         prep_we()
+        def live(c):
+            return 0 <= c < NCH
+
         for k in range(-1, NCH + 2):
-            for b in range(4):
-                if 0 <= k + 1 < NCH:
+            if live(k - 1):
+                relu_regroup(k - 1)
+            if live(k + 1):
+                for b in range(4):
                     xt_bank(k + 1, b)
-                if b == 0 and 0 <= k - 1 < NCH:
-                    relu_regroup(k - 1)
-                if 0 <= k - 2 < NCH:
-                    back(k - 2, b)
-                    if k - 2 == NCH - 1:
-                        store(k - 2, b, b + 1)
-                    if b == 0:
-                        sum_a(k - 2)
-                if b == 1 and 0 <= k - 1 < NCH:
-                    quant_h(k - 1)
-            if 0 <= k - 2 < NCH - 1:
-                store(k - 2, 0, 4)
+            if live(k - 2):
+                sum_a(k - 2, 0)
+            if live(k - 1):
+                quant_h(k - 1)
             if k == 0:
                 prep_we2_regroup()
-            for step in range(5):
-                if step < 4 and 0 <= k < NCH:
-                    stage1(k, step)
-                if step == 1 and 0 <= k + 1 < NCH:
-                    quant_x(k + 1)
-                if step > 0 and 0 <= k - 1 < NCH:
-                    stage2(k - 1, step - 1)
+            if live(k):
+                stage1(k, 0)
+                stage1(k, 1)
+            if live(k - 2):
+                for tl in range(4):
+                    back(k - 2, tl)
+                    if k - 2 == NCH - 1:
+                        store(k - 2, tl, tl + 1)
+                if k - 2 < NCH - 1:
+                    store(k - 2, 0, 4)
+            if live(k + 1):
+                quant_x(k + 1)
+            if live(k):
+                stage1(k, 2)
+                stage1(k, 3)
             if k == 0:
                 prep_we2_quant()
+            if live(k - 2):
+                for tl in range(4):
+                    accumulate(k - 2, tl)
+                sum_a(k - 2, 1)
+            if live(k - 1):
+                for m in range(4):
+                    stage2(k - 1, m)
 
         pa = bank("ps_suma")
         for m in range(4):

@@ -17,11 +17,12 @@ NA = 64
 NB = 64
 K1 = 1024
 ED = 512
-CH = 512
-NCH = NA * NB // CH
 FLOPS = 2 * NA * NB * K1 * ED + 2 * NA * NB * ED * ED
 
-MANUAL = True
+TILES = (2, 2, 4, 4, 4, 4, 4, 4, 2, 2)
+ACCUM_M = 1
+W_ON_SCALAR = False
+ACC_LAG = 3
 
 
 def tile_bipartiteneuralmessagepassinglayer_pa_t_kernel(
@@ -30,73 +31,85 @@ def tile_bipartiteneuralmessagepassinglayer_pa_t_kernel(
     nc = tc.nc
     x_rows = edge_embeds.rearrange("i j k -> (i j) k")
     o_rows = out_0.rearrange("i j f -> (i j) f")
+    NC = len(TILES)
+    first_tile = [sum(TILES[:c]) for c in range(NC)]
+    assert sum(TILES) * P == NA * NB
 
     with ExitStack() as ctx:
         const = ctx.enter_context(tc.tile_pool(name="const", bufs=1))
         work = ctx.enter_context(tc.tile_pool(name="work", bufs=2))
         psum = ctx.enter_context(tc.psum_pool(name="psum", bufs=7))
         psacc = ctx.enter_context(tc.psum_pool(name="psacc", bufs=1))
-        if MANUAL:
-            ctx.enter_context(tc.manual_schedule())
+        ctx.enter_context(tc.manual_schedule())
 
         def bank(label):
             return psum.tile([P, 512], F32, tag="bank", name=label)
 
-        ident = const.tile([P, P], F32, name="ident")
-        make_identity(nc, ident[:])
-        sel = const.tile([P, P], F32, name="sel")
-        nc.vector.tensor_tensor(out=sel[:, 0:NB], in0=ident[:, 0:NB], in1=ident[:, NB:P], op=ADD)
-        nc.vector.tensor_tensor(out=sel[:, NB:P], in0=ident[:, 0:NB], in1=ident[:, NB:P], op=ADD)
-        acc = psacc.tile([P, ED], F32, name="acc")
         ab_bf = const.tile([P, ED], BF16, name="ab_bf")
         bias_bf = const.tile([P, P], BF16, name="bias_bf")
-        st = const.tile([P, 4, P], F32, name="st")
         nc.vector.memset(bias_bf[:], 0.0)
-        nc.vector.memset(st[:], 0.0)
         nc.scalar.dma_start(out=ab_bf[0:NA, :], in_=a_proj)
         nc.scalar.dma_start(out=ab_bf[NA:P, :], in_=b_proj)
         nc.scalar.dma_start(out=bias_bf[0:4, :], in_=be1.rearrange("(m f) -> m f", m=4))
         nc.scalar.dma_start(out=bias_bf[4:8, :], in_=be2.rearrange("(m f) -> m f", m=4))
+        ident = const.tile([P, P], F32, name="ident")
+        make_identity(nc, ident[:])
+        acc = psacc.tile([P, ED], F32, name="acc")
 
         xs = []
-        for c in range(NCH):
-            xs.append(const.tile([P, 4, K1], BF16, name="x%d" % c))
+        for c in range(NC):
+            xs.append(const.tile([P, TILES[c], K1], BF16, name="x%d" % c))
         wraw = const.tile([P, 4, 2 * ED], BF16, name="wraw")
         w2raw = const.tile([P, 4, ED], BF16, name="w2raw")
         we_view = We.rearrange("(gu p e) c -> p gu (e c)", gu=4, p=P, e=2)
 
-        def load_x(c, t0, t1):
-            rows = x_rows[c * CH + t0 * P : c * CH + t1 * P, :]
-            nc.sync.dma_start(out=xs[c][:, t0:t1, :], in_=rows.rearrange("(t p) k -> p t k", p=P))
+        def load_x(c):
+            r0 = first_tile[c] * P
+            rows = x_rows[r0 : r0 + TILES[c] * P, :]
+            nc.sync.dma_start(out=xs[c][:], in_=rows.rearrange("(t p) k -> p t k", p=P))
 
-        nc.sync.dma_start(out=wraw[:, 0:2, :], in_=we_view[:, 0:2, :])
-        nc.sync.dma_start(out=wraw[:, 2:4, :], in_=we_view[:, 2:4, :])
-        load_x(0, 0, 2)
-        load_x(0, 2, 4)
-        load_x(1, 0, 4)
+        def load_w(g):
+            nc.sync.dma_start(out=wraw[:, 2 * g : 2 * g + 2, :], in_=we_view[:, 2 * g : 2 * g + 2, :])
+
+        load_w(0)
+        load_w(1)
+        load_x(0)
+        load_x(1)
         nc.sync.dma_start(out=w2raw[:], in_=We2.rearrange("(t p) c -> p t c", p=P))
-        for c in range(2, NCH):
-            load_x(c, 0, 4)
+        for c in range(2, NC):
+            load_x(c)
 
         ab32 = const.tile([P, ED], F32, name="ab32")
         bias32 = const.tile([P, P], F32, name="bias32")
-        nc.vector.tensor_copy(out=ab32[:], in_=ab_bf[:])
-        nc.vector.tensor_copy(out=bias32[:], in_=bias_bf[:])
-        ps_ab = bank("ps_ab")
-        for m in range(4):
-            nc.tensor.transpose(ps_ab[:, m * P : (m + 1) * P], ab32[:, m * P : (m + 1) * P], ident[:])
-        ps_bias = bank("ps_bias")
-        nc.tensor.transpose(ps_bias[:, 0:P], bias32[:], ident[:])
         biasT = const.tile([P, 8], F32, name="biasT")
         abT = const.tile([P, 4, P], F32, name="abT")
-        nc.vector.tensor_copy(out=biasT[:], in_=ps_bias[:, 0:8])
-        nc.vector.tensor_copy(
-            out=abT[:, :, 0:NA], in_=ps_ab[:].rearrange("p (m r) -> p m r", m=4)[:, :, 0:NA]
-        )
-        for m in range(4):
-            nc.vector.tensor_scalar_add(
-                out=abT[:, m, NA:P], in0=ps_ab[:, m * P + NA : (m + 1) * P], scalar1=biasT[:, m : m + 1]
+        st = const.tile([P, 4, P], F32, name="st")
+        sel = const.tile([P, P], F32, name="sel")
+
+        def small_inputs_cast():
+            nc.vector.tensor_copy(out=ab32[:], in_=ab_bf[:])
+            nc.vector.tensor_copy(out=bias32[:], in_=bias_bf[:])
+
+        def small_inputs_transpose():
+            ps_ab = bank("ps_ab")
+            for m in range(4):
+                nc.tensor.transpose(ps_ab[:, m * P : (m + 1) * P], ab32[:, m * P : (m + 1) * P], ident[:])
+            ps_bias = bank("ps_bias")
+            nc.tensor.transpose(ps_bias[:, 0:P], bias32[:], ident[:])
+            return ps_ab, ps_bias
+
+        def small_inputs_finish(ps_ab, ps_bias):
+            nc.vector.tensor_copy(out=biasT[:], in_=ps_bias[:, 0:8])
+            nc.vector.tensor_copy(
+                out=abT[:, :, 0:NA], in_=ps_ab[:].rearrange("p (m r) -> p m r", m=4)[:, :, 0:NA]
             )
+            for m in range(4):
+                nc.vector.tensor_scalar_add(
+                    out=abT[:, m, NA:P], in0=ps_ab[:, m * P + NA : (m + 1) * P], scalar1=biasT[:, m : m + 1]
+                )
+            nc.vector.memset(st[:], 0.0)
+            nc.vector.tensor_tensor(out=sel[:, 0:NB], in0=ident[:, 0:NB], in1=ident[:, NB:P], op=ADD)
+            nc.vector.tensor_tensor(out=sel[:, NB:P], in0=ident[:, 0:NB], in1=ident[:, NB:P], op=ADD)
 
         wg = const.tile([P, 2, ED, 4], BF16, name="wg", align_bytes=64)
         wq = const.tile([P, 2 * ED], U32, name="wq", align_bytes=64)
@@ -114,7 +127,7 @@ def tile_bipartiteneuralmessagepassinglayer_pa_t_kernel(
         def prep_we():
             for g in range(2):
                 src = wraw[:, 2 * g : 2 * g + 2, :].rearrange("p u (e c) -> p (u e) c", e=2)
-                regroup(nc.vector.tensor_copy, wg[:, g, :, :], src)
+                regroup(nc.scalar.copy if (g == 1 and W_ON_SCALAR) else nc.vector.tensor_copy, wg[:, g, :, :], src)
             nc.vector.quantize_mx(
                 out=wq[:].bitcast(FP8X4),
                 scales=wsc[:],
@@ -139,29 +152,32 @@ def tile_bipartiteneuralmessagepassinglayer_pa_t_kernel(
         lt = {}
         lo = {}
 
-        def xt_bank(c, b):
-            g = b // 2
-            eh = b % 2
-            if b == 0:
-                xg[c] = work.tile([P, 2, CH, 2], F32, name="xg%d" % c, tag="xg", align_bytes=64)
-            pb = bank("xt%d_%d" % (c, b))
-            for u in range(2):
-                for tl in range(2):
-                    words = xs[c][:, 2 * eh + tl, :].bitcast(F32)
-                    nc.tensor.transpose(
-                        pb[:, u * 256 + tl * P : u * 256 + (tl + 1) * P],
-                        words[:, 256 * g + P * u : 256 * g + P * (u + 1)],
-                        ident[:],
+        def live(c):
+            return 0 <= c < NC
+
+        def transpose_x(c):
+            n = TILES[c] * P
+            xg[c] = work.tile([P, 2, n, 2], F32, name="xg%d" % c, tag="xg", align_bytes=64)
+            for eh in range(TILES[c] // 2):
+                for g in range(2):
+                    pb = bank("xt%d_%d_%d" % (c, g, eh))
+                    for u in range(2):
+                        for tl in range(2):
+                            words = xs[c][:, 2 * eh + tl, :].bitcast(F32)
+                            nc.tensor.transpose(
+                                pb[:, u * 256 + tl * P : u * 256 + (tl + 1) * P],
+                                words[:, 256 * g + P * u : 256 * g + P * (u + 1)],
+                                ident[:],
+                            )
+                    nc.scalar.copy(
+                        out=xg[c][:, g, eh * 256 : (eh + 1) * 256, :],
+                        in_=pb[:].rearrange("p (u e) -> p e u", u=2),
                     )
-            copy_out = nc.vector.tensor_copy if (c == 0 and g == 1) else nc.scalar.copy
-            copy_out(
-                out=xg[c][:, g, eh * 256 : (eh + 1) * 256, :],
-                in_=pb[:].rearrange("p (u e) -> p e u", u=2),
-            )
 
         def quant_x(c):
-            xq[c] = work.tile([P, 2 * CH], U32, name="xq%d" % c, tag="xq", align_bytes=64)
-            xsc[c] = work.tile([P, 2 * CH], U8, name="xsc%d" % c, tag="xsc", align_bytes=64)
+            n = TILES[c] * P
+            xq[c] = work.tile([P, 2 * n], U32, name="xq%d" % c, tag="xq", align_bytes=64)
+            xsc[c] = work.tile([P, 2 * n], U8, name="xsc%d" % c, tag="xsc", align_bytes=64)
             nc.vector.quantize_mx(
                 out=xq[c][:].bitcast(FP8X4),
                 scales=xsc[c][:],
@@ -169,22 +185,23 @@ def tile_bipartiteneuralmessagepassinglayer_pa_t_kernel(
             )
 
         def stage1(c, m):
+            n = TILES[c] * P
             if m == 0:
-                yy[c] = work.tile([P, 4, CH], BF16, name="y%d" % c, tag="y")
+                yy[c] = work.tile([P, 4, n], BF16, name="y%d" % c, tag="y")
             pb = bank("p1_%d_%d" % (c, m))
             for g in range(2):
                 cols = slice(g * ED + m * P, g * ED + (m + 1) * P)
                 nc.tensor.matmul_mx(
-                    out=pb[:],
+                    out=pb[:, 0:n],
                     lhsT=wq[:, cols].bitcast(FP8X4),
                     lhsT_scale=wsc[:, cols],
-                    rhs=xq[c][:, g * CH : (g + 1) * CH].bitcast(FP8X4),
-                    rhs_scale=xsc[c][:, g * CH : (g + 1) * CH],
+                    rhs=xq[c][:, g * n : (g + 1) * n].bitcast(FP8X4),
+                    rhs_scale=xsc[c][:, g * n : (g + 1) * n],
                     start=(g == 0),
                     stop=(g == 1),
                 )
-            for il in range(8):
-                i = 8 * c + il
+            for il in range(2 * TILES[c]):
+                i = 2 * first_tile[c] + il
                 nc.vector.scalar_tensor_tensor(
                     out=yy[c][:, m, il * NB : (il + 1) * NB],
                     in0=pb[:, il * NB : (il + 1) * NB],
@@ -195,7 +212,8 @@ def tile_bipartiteneuralmessagepassinglayer_pa_t_kernel(
                 )
 
         def relu_regroup(c):
-            hg[c] = work.tile([P, CH, 4], BF16, name="hg%d" % c, tag="hg", align_bytes=64)
+            n = TILES[c] * P
+            hg[c] = work.tile([P, n, 4], BF16, name="hg%d" % c, tag="hg", align_bytes=64)
             nc.vector.tensor_scalar_max(
                 out=hg[c][:].rearrange("p (c i) t -> p c t i", i=4),
                 in0=yy[c][:].rearrange("p t (c i) -> p c t i", i=4),
@@ -203,8 +221,9 @@ def tile_bipartiteneuralmessagepassinglayer_pa_t_kernel(
             )
 
         def quant_h(c):
-            hq[c] = work.tile([P, CH], U32, name="hq%d" % c, tag="hq", align_bytes=64)
-            hsc[c] = work.tile([P, CH], U8, name="hsc%d" % c, tag="hsc", align_bytes=64)
+            n = TILES[c] * P
+            hq[c] = work.tile([P, n], U32, name="hq%d" % c, tag="hq", align_bytes=64)
+            hsc[c] = work.tile([P, n], U8, name="hsc%d" % c, tag="hsc", align_bytes=64)
             nc.vector.quantize_mx(
                 out=hq[c][:].bitcast(FP8X4),
                 scales=hsc[c][:],
@@ -212,12 +231,13 @@ def tile_bipartiteneuralmessagepassinglayer_pa_t_kernel(
             )
 
         def stage2(c, m):
+            n = TILES[c] * P
             if m == 0:
-                lt[c] = work.tile([P, 4, CH], F32, name="lt%d" % c, tag="lt", bufs=3)
+                lt[c] = work.tile([P, 4, n], F32, name="lt%d" % c, tag="lt", bufs=ACC_LAG)
             pb = bank("p2_%d_%d" % (c, m))
             cols = slice(m * P, (m + 1) * P)
             nc.tensor.matmul_mx(
-                out=pb[:],
+                out=pb[:, 0:n],
                 lhsT=w2q[:, cols].bitcast(FP8X4),
                 lhsT_scale=w2sc[:, cols],
                 rhs=hq[c][:].bitcast(FP8X4),
@@ -225,54 +245,76 @@ def tile_bipartiteneuralmessagepassinglayer_pa_t_kernel(
                 start=True,
                 stop=True,
             )
-            nc.scalar.activation(
-                out=lt[c][:, m, :], in_=pb[:], func=RELU, bias=biasT[:, 4 + m : 5 + m], scale=1.0
-            )
+            if m < 4 - ACCUM_M:
+                nc.scalar.activation(
+                    out=lt[c][:, m, :], in_=pb[:, 0:n], func=RELU, bias=biasT[:, 4 + m : 5 + m], scale=1.0
+                )
+            else:
+                for il in range(2 * TILES[c]):
+                    i = 2 * first_tile[c] + il
+                    nc.scalar.activation(
+                        out=lt[c][:, m, il * NB : (il + 1) * NB],
+                        in_=pb[:, il * NB : (il + 1) * NB],
+                        func=RELU,
+                        bias=biasT[:, 4 + m : 5 + m],
+                        scale=1.0,
+                        accum_out=st[:, m, i : i + 1],
+                    )
 
         def sum_a(c, half):
-            ms = slice(2 * half, 2 * half + 2)
+            ms = slice(2 * half, min(2 * half + 2, 4 - ACCUM_M))
+            i0 = 2 * first_tile[c]
             nc.vector.tensor_reduce(
-                out=st[:, ms, 8 * c : 8 * c + 8],
+                out=st[:, ms, i0 : i0 + 2 * TILES[c]],
                 in_=lt[c][:, ms, :].rearrange("p m (i j) -> p m i j", j=NB),
                 axis=AX_X,
                 op=ADD,
             )
 
-        def back(c, tl):
-            if tl == 0:
-                lo[c] = work.tile([P, 4, ED], F32, name="lo%d" % c, tag="lo")
-            pb = bank("lb%d_%d" % (c, tl))
-            for m in range(4):
-                nc.tensor.transpose(
-                    pb[:, m * P : (m + 1) * P], lt[c][:, m, tl * P : (tl + 1) * P], ident[:]
-                )
-            nc.scalar.copy(out=lo[c][:, tl, :], in_=pb[:])
+        def back(c):
+            lo[c] = work.tile([P, TILES[c], ED], F32, name="lo%d" % c, tag="lo")
+            r0 = first_tile[c] * P
+            for tl in range(TILES[c]):
+                pb = bank("lb%d_%d" % (c, tl))
+                for m in range(4):
+                    nc.tensor.transpose(
+                        pb[:, m * P : (m + 1) * P], lt[c][:, m, tl * P : (tl + 1) * P], ident[:]
+                    )
+                nc.scalar.copy(out=lo[c][:, tl, :], in_=pb[:])
+                if c == NC - 1:
+                    nc.sync.dma_start(out=o_rows[r0 + tl * P : r0 + (tl + 1) * P, :], in_=lo[c][:, tl, :])
+            if c < NC - 1:
+                rows = o_rows[r0 : r0 + TILES[c] * P, :]
+                nc.sync.dma_start(out=rows.rearrange("(t p) f -> p t f", p=P), in_=lo[c][:])
 
-        def accumulate(c, tl):
-            for m in range(4):
-                nc.tensor.matmul(
-                    out=acc[:, m * P : (m + 1) * P],
-                    lhsT=lt[c][:, m, tl * P : (tl + 1) * P],
-                    rhs=ident[:],
-                    is_transpose=True,
-                    start=(c == 0 and tl == 0 and m == 0),
-                    stop=(c == NCH - 1 and tl == 3 and m == 3),
-                )
-
-        def store(c, t0, t1):
-            rows = o_rows[c * CH + t0 * P : c * CH + t1 * P, :]
-            nc.sync.dma_start(out=rows.rearrange("(t p) f -> p t f", p=P), in_=lo[c][:, t0:t1, :])
+        def accumulate(c):
+            for tl in range(TILES[c]):
+                for m in range(4):
+                    nc.tensor.matmul(
+                        out=acc[:, m * P : (m + 1) * P],
+                        lhsT=lt[c][:, m, tl * P : (tl + 1) * P],
+                        rhs=ident[:],
+                        is_transpose=True,
+                        start=(c == 0 and tl == 0 and m == 0),
+                        stop=(c == NC - 1 and tl == TILES[c] - 1 and m == 3),
+                    )
 
         prep_we()
-        def live(c):
-            return 0 <= c < NCH
-
-        for k in range(-1, NCH + 2):
+        transpose_x(0)
+        small_inputs_cast()
+        ps_small = small_inputs_transpose()
+        quant_x(0)
+        small_inputs_finish(ps_small[0], ps_small[1])
+        for k in range(NC + 2):
             if live(k - 1):
                 relu_regroup(k - 1)
             if live(k + 1):
-                for b in range(4):
-                    xt_bank(k + 1, b)
+                transpose_x(k + 1)
+            if live(k - ACC_LAG):
+                accumulate(k - ACC_LAG)
+            if k == NC + 1:
+                for c in range(k - ACC_LAG + 1, NC):
+                    accumulate(c)
             if live(k - 2):
                 sum_a(k - 2, 0)
             if live(k - 1):
@@ -283,12 +325,7 @@ def tile_bipartiteneuralmessagepassinglayer_pa_t_kernel(
                 stage1(k, 0)
                 stage1(k, 1)
             if live(k - 2):
-                for tl in range(4):
-                    back(k - 2, tl)
-                    if k - 2 == NCH - 1:
-                        store(k - 2, tl, tl + 1)
-                if k - 2 < NCH - 1:
-                    store(k - 2, 0, 4)
+                back(k - 2)
             if live(k + 1):
                 quant_x(k + 1)
             if live(k):
@@ -296,13 +333,11 @@ def tile_bipartiteneuralmessagepassinglayer_pa_t_kernel(
                 stage1(k, 3)
             if k == 0:
                 prep_we2_quant()
-            if live(k - 2):
-                for tl in range(4):
-                    accumulate(k - 2, tl)
-                sum_a(k - 2, 1)
             if live(k - 1):
                 for m in range(4):
                     stage2(k - 1, m)
+            if live(k - 2):
+                sum_a(k - 2, 1)
 
         pa = bank("ps_suma")
         for m in range(4):

@@ -17,11 +17,11 @@ NA = 64
 NB = 64
 K1 = 1024
 ED = 512
+BLOCKS = ED // P
 FLOPS = 2 * NA * NB * K1 * ED + 2 * NA * NB * ED * ED
 
 TILES = (2, 2, 4, 4, 4, 4, 4, 4, 2, 2)
-ACCUM_M = 1
-W_ON_SCALAR = False
+VECTOR_SUM_BLOCKS = 4
 ACC_LAG = 3
 
 
@@ -50,8 +50,8 @@ def tile_bipartiteneuralmessagepassinglayer_pa_t_kernel(
         nc.vector.memset(bias_bf[:], 0.0)
         nc.scalar.dma_start(out=ab_bf[0:NA, :], in_=a_proj)
         nc.scalar.dma_start(out=ab_bf[NA:P, :], in_=b_proj)
-        nc.scalar.dma_start(out=bias_bf[0:4, :], in_=be1.rearrange("(m f) -> m f", m=4))
-        nc.scalar.dma_start(out=bias_bf[4:8, :], in_=be2.rearrange("(m f) -> m f", m=4))
+        nc.scalar.dma_start(out=bias_bf[0:4, :], in_=be1.rearrange("(m f) -> m f", m=BLOCKS))
+        nc.scalar.dma_start(out=bias_bf[4:8, :], in_=be2.rearrange("(m f) -> m f", m=BLOCKS))
         ident = const.tile([P, P], F32, name="ident")
         make_identity(nc, ident[:])
         acc = psacc.tile([P, ED], F32, name="acc")
@@ -82,8 +82,8 @@ def tile_bipartiteneuralmessagepassinglayer_pa_t_kernel(
         ab32 = const.tile([P, ED], F32, name="ab32")
         bias32 = const.tile([P, P], F32, name="bias32")
         biasT = const.tile([P, 8], F32, name="biasT")
-        abT = const.tile([P, 4, P], F32, name="abT")
-        st = const.tile([P, 4, P], F32, name="st")
+        abT = const.tile([P, BLOCKS, P], F32, name="abT")
+        st = const.tile([P, BLOCKS, P], F32, name="st")
         sel = const.tile([P, P], F32, name="sel")
 
         def small_inputs_cast():
@@ -92,7 +92,7 @@ def tile_bipartiteneuralmessagepassinglayer_pa_t_kernel(
 
         def small_inputs_transpose():
             ps_ab = bank("ps_ab")
-            for m in range(4):
+            for m in range(BLOCKS):
                 nc.tensor.transpose(ps_ab[:, m * P : (m + 1) * P], ab32[:, m * P : (m + 1) * P], ident[:])
             ps_bias = bank("ps_bias")
             nc.tensor.transpose(ps_bias[:, 0:P], bias32[:], ident[:])
@@ -101,9 +101,9 @@ def tile_bipartiteneuralmessagepassinglayer_pa_t_kernel(
         def small_inputs_finish(ps_ab, ps_bias):
             nc.vector.tensor_copy(out=biasT[:], in_=ps_bias[:, 0:8])
             nc.vector.tensor_copy(
-                out=abT[:, :, 0:NA], in_=ps_ab[:].rearrange("p (m r) -> p m r", m=4)[:, :, 0:NA]
+                out=abT[:, :, 0:NA], in_=ps_ab[:].rearrange("p (m r) -> p m r", m=BLOCKS)[:, :, 0:NA]
             )
-            for m in range(4):
+            for m in range(BLOCKS):
                 nc.vector.tensor_scalar_add(
                     out=abT[:, m, NA:P], in0=ps_ab[:, m * P + NA : (m + 1) * P], scalar1=biasT[:, m : m + 1]
                 )
@@ -118,8 +118,8 @@ def tile_bipartiteneuralmessagepassinglayer_pa_t_kernel(
         w2q = const.tile([P, ED], U32, name="w2q", align_bytes=64)
         w2sc = const.tile([P, ED], U8, name="w2sc", align_bytes=64)
 
-        def regroup(eng_copy, dst, src):
-            eng_copy(
+        def regroup(copy, dst, src):
+            copy(
                 out=dst.rearrange("p (c i) t -> p c t i", i=4),
                 in_=src.rearrange("p t (c i) -> p c t i", i=4),
             )
@@ -127,7 +127,7 @@ def tile_bipartiteneuralmessagepassinglayer_pa_t_kernel(
         def prep_we():
             for g in range(2):
                 src = wraw[:, 2 * g : 2 * g + 2, :].rearrange("p u (e c) -> p (u e) c", e=2)
-                regroup(nc.scalar.copy if (g == 1 and W_ON_SCALAR) else nc.vector.tensor_copy, wg[:, g, :, :], src)
+                regroup(nc.vector.tensor_copy, wg[:, g, :, :], src)
             nc.vector.quantize_mx(
                 out=wq[:].bitcast(FP8X4),
                 scales=wsc[:],
@@ -187,7 +187,7 @@ def tile_bipartiteneuralmessagepassinglayer_pa_t_kernel(
         def stage1(c, m):
             n = TILES[c] * P
             if m == 0:
-                yy[c] = work.tile([P, 4, n], BF16, name="y%d" % c, tag="y")
+                yy[c] = work.tile([P, BLOCKS, n], BF16, name="y%d" % c, tag="y")
             pb = bank("p1_%d_%d" % (c, m))
             for g in range(2):
                 cols = slice(g * ED + m * P, g * ED + (m + 1) * P)
@@ -233,7 +233,7 @@ def tile_bipartiteneuralmessagepassinglayer_pa_t_kernel(
         def stage2(c, m):
             n = TILES[c] * P
             if m == 0:
-                lt[c] = work.tile([P, 4, n], F32, name="lt%d" % c, tag="lt", bufs=ACC_LAG)
+                lt[c] = work.tile([P, BLOCKS, n], F32, name="lt%d" % c, tag="lt", bufs=ACC_LAG)
             pb = bank("p2_%d_%d" % (c, m))
             cols = slice(m * P, (m + 1) * P)
             nc.tensor.matmul_mx(
@@ -245,7 +245,7 @@ def tile_bipartiteneuralmessagepassinglayer_pa_t_kernel(
                 start=True,
                 stop=True,
             )
-            if m < 4 - ACCUM_M:
+            if m < VECTOR_SUM_BLOCKS:
                 nc.scalar.activation(
                     out=lt[c][:, m, :], in_=pb[:, 0:n], func=RELU, bias=biasT[:, 4 + m : 5 + m], scale=1.0
                 )
@@ -261,12 +261,11 @@ def tile_bipartiteneuralmessagepassinglayer_pa_t_kernel(
                         accum_out=st[:, m, i : i + 1],
                     )
 
-        def sum_a(c, half):
-            ms = slice(2 * half, min(2 * half + 2, 4 - ACCUM_M))
+        def sum_a(c, m0, m1):
             i0 = 2 * first_tile[c]
             nc.vector.tensor_reduce(
-                out=st[:, ms, i0 : i0 + 2 * TILES[c]],
-                in_=lt[c][:, ms, :].rearrange("p m (i j) -> p m i j", j=NB),
+                out=st[:, m0:m1, i0 : i0 + 2 * TILES[c]],
+                in_=lt[c][:, m0:m1, :].rearrange("p m (i j) -> p m i j", j=NB),
                 axis=AX_X,
                 op=ADD,
             )
@@ -276,7 +275,7 @@ def tile_bipartiteneuralmessagepassinglayer_pa_t_kernel(
             r0 = first_tile[c] * P
             for tl in range(TILES[c]):
                 pb = bank("lb%d_%d" % (c, tl))
-                for m in range(4):
+                for m in range(BLOCKS):
                     nc.tensor.transpose(
                         pb[:, m * P : (m + 1) * P], lt[c][:, m, tl * P : (tl + 1) * P], ident[:]
                     )
@@ -289,14 +288,14 @@ def tile_bipartiteneuralmessagepassinglayer_pa_t_kernel(
 
         def accumulate(c):
             for tl in range(TILES[c]):
-                for m in range(4):
+                for m in range(BLOCKS):
                     nc.tensor.matmul(
                         out=acc[:, m * P : (m + 1) * P],
                         lhsT=lt[c][:, m, tl * P : (tl + 1) * P],
                         rhs=ident[:],
                         is_transpose=True,
                         start=(c == 0 and tl == 0 and m == 0),
-                        stop=(c == NC - 1 and tl == TILES[c] - 1 and m == 3),
+                        stop=(c == NC - 1 and tl == TILES[c] - 1 and m == BLOCKS - 1),
                     )
 
         prep_we()
@@ -316,7 +315,7 @@ def tile_bipartiteneuralmessagepassinglayer_pa_t_kernel(
                 for c in range(k - ACC_LAG + 1, NC):
                     accumulate(c)
             if live(k - 2):
-                sum_a(k - 2, 0)
+                sum_a(k - 2, 0, 2)
             if live(k - 1):
                 quant_h(k - 1)
             if k == 0:
@@ -334,13 +333,13 @@ def tile_bipartiteneuralmessagepassinglayer_pa_t_kernel(
             if k == 0:
                 prep_we2_quant()
             if live(k - 1):
-                for m in range(4):
+                for m in range(BLOCKS):
                     stage2(k - 1, m)
             if live(k - 2):
-                sum_a(k - 2, 1)
+                sum_a(k - 2, 2, VECTOR_SUM_BLOCKS)
 
         pa = bank("ps_suma")
-        for m in range(4):
+        for m in range(BLOCKS):
             nc.tensor.transpose(pa[:, m * P : (m + 1) * P], st[:, m, :], ident[:])
         so_a = const.tile([P, ED], F32, name="so_a")
         nc.scalar.copy(out=so_a[:], in_=pa[:])

@@ -18,10 +18,14 @@ NB = 64
 K1 = 1024
 ED = 512
 BLOCKS = ED // P
+PACK = 4
+PASSES = K1 // (P * PACK)
+BANK = 512
+PAIR = 2 * P
 FLOPS = 2 * NA * NB * K1 * ED + 2 * NA * NB * ED * ED
 
 TILES = (2, 2, 4, 4, 4, 4, 4, 4, 2, 2)
-VECTOR_SUM_BLOCKS = 4
+VECTOR_SUM_BLOCKS = 3
 ACC_LAG = 3
 
 
@@ -43,25 +47,30 @@ def tile_bipartiteneuralmessagepassinglayer_pa_t_kernel(
         ctx.enter_context(tc.manual_schedule())
 
         def bank(label):
-            return psum.tile([P, 512], F32, tag="bank", name=label)
+            return psum.tile([P, BANK], F32, tag="bank", name=label)
 
         ab_bf = const.tile([P, ED], BF16, name="ab_bf")
         bias_bf = const.tile([P, P], BF16, name="bias_bf")
         nc.vector.memset(bias_bf[:], 0.0)
         nc.scalar.dma_start(out=ab_bf[0:NA, :], in_=a_proj)
         nc.scalar.dma_start(out=ab_bf[NA:P, :], in_=b_proj)
-        nc.scalar.dma_start(out=bias_bf[0:4, :], in_=be1.rearrange("(m f) -> m f", m=BLOCKS))
-        nc.scalar.dma_start(out=bias_bf[4:8, :], in_=be2.rearrange("(m f) -> m f", m=BLOCKS))
+        nc.scalar.dma_start(out=bias_bf[0:BLOCKS, :], in_=be1.rearrange("(m f) -> m f", m=BLOCKS))
+        nc.scalar.dma_start(out=bias_bf[BLOCKS : 2 * BLOCKS, :], in_=be2.rearrange("(m f) -> m f", m=BLOCKS))
         ident = const.tile([P, P], F32, name="ident")
         make_identity(nc, ident[:])
         acc = psacc.tile([P, ED], F32, name="acc")
+        st = const.tile([P, BLOCKS, P], F32, name="st")
+        sel = const.tile([P, P], F32, name="sel")
+        nc.gpsimd.memset(st[:], 0.0)
+        nc.gpsimd.tensor_tensor(out=sel[:, 0:NB], in0=ident[:, 0:NB], in1=ident[:, NB:P], op=ADD)
+        nc.gpsimd.tensor_tensor(out=sel[:, NB:P], in0=ident[:, 0:NB], in1=ident[:, NB:P], op=ADD)
 
         xs = []
         for c in range(NC):
             xs.append(const.tile([P, TILES[c], K1], BF16, name="x%d" % c))
-        wraw = const.tile([P, 4, 2 * ED], BF16, name="wraw")
-        w2raw = const.tile([P, 4, ED], BF16, name="w2raw")
-        we_view = We.rearrange("(gu p e) c -> p gu (e c)", gu=4, p=P, e=2)
+        wraw = const.tile([P, 2 * PASSES, 2 * ED], BF16, name="wraw")
+        w2raw = const.tile([P, PACK, ED], BF16, name="w2raw")
+        we_view = We.rearrange("(gu p v) c -> p gu (v c)", gu=2 * PASSES, p=P, v=2)
 
         def load_x(c):
             r0 = first_tile[c] * P
@@ -81,14 +90,12 @@ def tile_bipartiteneuralmessagepassinglayer_pa_t_kernel(
 
         ab32 = const.tile([P, ED], F32, name="ab32")
         bias32 = const.tile([P, P], F32, name="bias32")
-        biasT = const.tile([P, 8], F32, name="biasT")
+        biasT = const.tile([P, 2 * BLOCKS], F32, name="biasT")
         abT = const.tile([P, BLOCKS, P], F32, name="abT")
-        st = const.tile([P, BLOCKS, P], F32, name="st")
-        sel = const.tile([P, P], F32, name="sel")
 
         def small_inputs_cast():
-            nc.vector.tensor_copy(out=ab32[:], in_=ab_bf[:])
-            nc.vector.tensor_copy(out=bias32[:], in_=bias_bf[:])
+            nc.scalar.copy(out=ab32[:], in_=ab_bf[:])
+            nc.scalar.copy(out=bias32[:], in_=bias_bf[:])
 
         def small_inputs_transpose():
             ps_ab = bank("ps_ab")
@@ -99,7 +106,7 @@ def tile_bipartiteneuralmessagepassinglayer_pa_t_kernel(
             return ps_ab, ps_bias
 
         def small_inputs_finish(ps_ab, ps_bias):
-            nc.vector.tensor_copy(out=biasT[:], in_=ps_bias[:, 0:8])
+            nc.vector.tensor_copy(out=biasT[:], in_=ps_bias[:, 0 : 2 * BLOCKS])
             nc.vector.tensor_copy(
                 out=abT[:, :, 0:NA], in_=ps_ab[:].rearrange("p (m r) -> p m r", m=BLOCKS)[:, :, 0:NA]
             )
@@ -107,26 +114,23 @@ def tile_bipartiteneuralmessagepassinglayer_pa_t_kernel(
                 nc.vector.tensor_scalar_add(
                     out=abT[:, m, NA:P], in0=ps_ab[:, m * P + NA : (m + 1) * P], scalar1=biasT[:, m : m + 1]
                 )
-            nc.vector.memset(st[:], 0.0)
-            nc.vector.tensor_tensor(out=sel[:, 0:NB], in0=ident[:, 0:NB], in1=ident[:, NB:P], op=ADD)
-            nc.vector.tensor_tensor(out=sel[:, NB:P], in0=ident[:, 0:NB], in1=ident[:, NB:P], op=ADD)
 
-        wg = const.tile([P, 2, ED, 4], BF16, name="wg", align_bytes=64)
-        wq = const.tile([P, 2 * ED], U32, name="wq", align_bytes=64)
-        wsc = const.tile([P, 2 * ED], U8, name="wsc", align_bytes=64)
-        w2g = const.tile([P, ED, 4], BF16, name="w2g", align_bytes=64)
+        wg = const.tile([P, PASSES, ED, PACK], BF16, name="wg", align_bytes=64)
+        wq = const.tile([P, PASSES * ED], U32, name="wq", align_bytes=64)
+        wsc = const.tile([P, PASSES * ED], U8, name="wsc", align_bytes=64)
+        w2g = const.tile([P, ED, PACK], BF16, name="w2g", align_bytes=64)
         w2q = const.tile([P, ED], U32, name="w2q", align_bytes=64)
         w2sc = const.tile([P, ED], U8, name="w2sc", align_bytes=64)
 
-        def regroup(copy, dst, src):
-            copy(
-                out=dst.rearrange("p (c i) t -> p c t i", i=4),
-                in_=src.rearrange("p t (c i) -> p c t i", i=4),
+        def regroup(eng_copy, dst, src):
+            eng_copy(
+                out=dst.rearrange("p (c z) t -> p c t z", z=4),
+                in_=src.rearrange("p t (c z) -> p c t z", z=4),
             )
 
         def prep_we():
-            for g in range(2):
-                src = wraw[:, 2 * g : 2 * g + 2, :].rearrange("p u (e c) -> p (u e) c", e=2)
+            for g in range(PASSES):
+                src = wraw[:, 2 * g : 2 * g + 2, :].rearrange("p u (v c) -> p (u v) c", v=2)
                 regroup(nc.vector.tensor_copy, wg[:, g, :, :], src)
             nc.vector.quantize_mx(
                 out=wq[:].bitcast(FP8X4),
@@ -157,27 +161,27 @@ def tile_bipartiteneuralmessagepassinglayer_pa_t_kernel(
 
         def transpose_x(c):
             n = TILES[c] * P
-            xg[c] = work.tile([P, 2, n, 2], F32, name="xg%d" % c, tag="xg", align_bytes=64)
-            for eh in range(TILES[c] // 2):
-                for g in range(2):
-                    pb = bank("xt%d_%d_%d" % (c, g, eh))
+            xg[c] = work.tile([P, PASSES, n, 2], F32, name="xg%d" % c, tag="xg", align_bytes=64)
+            for pair in range(TILES[c] // 2):
+                for g in range(PASSES):
+                    pb = bank("xt%d_%d_%d" % (c, g, pair))
                     for u in range(2):
-                        for tl in range(2):
-                            words = xs[c][:, 2 * eh + tl, :].bitcast(F32)
+                        for side in range(2):
+                            words = xs[c][:, 2 * pair + side, :].bitcast(F32)
                             nc.tensor.transpose(
-                                pb[:, u * 256 + tl * P : u * 256 + (tl + 1) * P],
-                                words[:, 256 * g + P * u : 256 * g + P * (u + 1)],
+                                pb[:, u * PAIR + side * P : u * PAIR + (side + 1) * P],
+                                words[:, 2 * P * g + P * u : 2 * P * g + P * (u + 1)],
                                 ident[:],
                             )
                     nc.scalar.copy(
-                        out=xg[c][:, g, eh * 256 : (eh + 1) * 256, :],
+                        out=xg[c][:, g, pair * PAIR : (pair + 1) * PAIR, :],
                         in_=pb[:].rearrange("p (u e) -> p e u", u=2),
                     )
 
         def quant_x(c):
             n = TILES[c] * P
-            xq[c] = work.tile([P, 2 * n], U32, name="xq%d" % c, tag="xq", align_bytes=64)
-            xsc[c] = work.tile([P, 2 * n], U8, name="xsc%d" % c, tag="xsc", align_bytes=64)
+            xq[c] = work.tile([P, PASSES * n], U32, name="xq%d" % c, tag="xq", align_bytes=64)
+            xsc[c] = work.tile([P, PASSES * n], U8, name="xsc%d" % c, tag="xsc", align_bytes=64)
             nc.vector.quantize_mx(
                 out=xq[c][:].bitcast(FP8X4),
                 scales=xsc[c][:],
@@ -189,7 +193,7 @@ def tile_bipartiteneuralmessagepassinglayer_pa_t_kernel(
             if m == 0:
                 yy[c] = work.tile([P, BLOCKS, n], BF16, name="y%d" % c, tag="y")
             pb = bank("p1_%d_%d" % (c, m))
-            for g in range(2):
+            for g in range(PASSES):
                 cols = slice(g * ED + m * P, g * ED + (m + 1) * P)
                 nc.tensor.matmul_mx(
                     out=pb[:, 0:n],
@@ -198,7 +202,7 @@ def tile_bipartiteneuralmessagepassinglayer_pa_t_kernel(
                     rhs=xq[c][:, g * n : (g + 1) * n].bitcast(FP8X4),
                     rhs_scale=xsc[c][:, g * n : (g + 1) * n],
                     start=(g == 0),
-                    stop=(g == 1),
+                    stop=(g == PASSES - 1),
                 )
             for il in range(2 * TILES[c]):
                 i = 2 * first_tile[c] + il
@@ -213,10 +217,10 @@ def tile_bipartiteneuralmessagepassinglayer_pa_t_kernel(
 
         def relu_regroup(c):
             n = TILES[c] * P
-            hg[c] = work.tile([P, n, 4], BF16, name="hg%d" % c, tag="hg", align_bytes=64)
+            hg[c] = work.tile([P, n, PACK], BF16, name="hg%d" % c, tag="hg", align_bytes=64)
             nc.vector.tensor_scalar_max(
-                out=hg[c][:].rearrange("p (c i) t -> p c t i", i=4),
-                in0=yy[c][:].rearrange("p t (c i) -> p c t i", i=4),
+                out=hg[c][:].rearrange("p (c z) t -> p c t z", z=4),
+                in0=yy[c][:].rearrange("p t (c z) -> p c t z", z=4),
                 scalar1=0.0,
             )
 
@@ -247,7 +251,7 @@ def tile_bipartiteneuralmessagepassinglayer_pa_t_kernel(
             )
             if m < VECTOR_SUM_BLOCKS:
                 nc.scalar.activation(
-                    out=lt[c][:, m, :], in_=pb[:, 0:n], func=RELU, bias=biasT[:, 4 + m : 5 + m], scale=1.0
+                    out=lt[c][:, m, :], in_=pb[:, 0:n], func=RELU, bias=biasT[:, BLOCKS + m : BLOCKS + m + 1], scale=1.0
                 )
             else:
                 for il in range(2 * TILES[c]):
@@ -256,7 +260,7 @@ def tile_bipartiteneuralmessagepassinglayer_pa_t_kernel(
                         out=lt[c][:, m, il * NB : (il + 1) * NB],
                         in_=pb[:, il * NB : (il + 1) * NB],
                         func=RELU,
-                        bias=biasT[:, 4 + m : 5 + m],
+                        bias=biasT[:, BLOCKS + m : BLOCKS + m + 1],
                         scale=1.0,
                         accum_out=st[:, m, i : i + 1],
                     )
@@ -298,9 +302,9 @@ def tile_bipartiteneuralmessagepassinglayer_pa_t_kernel(
                         stop=(c == NC - 1 and tl == TILES[c] - 1 and m == BLOCKS - 1),
                     )
 
+        small_inputs_cast()
         prep_we()
         transpose_x(0)
-        small_inputs_cast()
         ps_small = small_inputs_transpose()
         quant_x(0)
         small_inputs_finish(ps_small[0], ps_small[1])
@@ -325,11 +329,11 @@ def tile_bipartiteneuralmessagepassinglayer_pa_t_kernel(
                 stage1(k, 1)
             if live(k - 2):
                 back(k - 2)
-            if live(k + 1):
-                quant_x(k + 1)
             if live(k):
                 stage1(k, 2)
                 stage1(k, 3)
+            if live(k + 1):
+                quant_x(k + 1)
             if k == 0:
                 prep_we2_quant()
             if live(k - 1):

@@ -59,11 +59,6 @@ def tile_bipartiteneuralmessagepassinglayer_pa_t_kernel(
         ident = const.tile([P, P], F32, name="ident")
         make_identity(nc, ident[:])
         acc = psacc.tile([P, ED], F32, name="acc")
-        st = const.tile([P, BLOCKS, P], F32, name="st")
-        sel = const.tile([P, P], F32, name="sel")
-        nc.gpsimd.memset(st[:], 0.0)
-        nc.gpsimd.tensor_tensor(out=sel[:, 0:NB], in0=ident[:, 0:NB], in1=ident[:, NB:P], op=ADD)
-        nc.gpsimd.tensor_tensor(out=sel[:, NB:P], in0=ident[:, 0:NB], in1=ident[:, NB:P], op=ADD)
 
         xs = []
         for c in range(NC):
@@ -92,10 +87,12 @@ def tile_bipartiteneuralmessagepassinglayer_pa_t_kernel(
         bias32 = const.tile([P, P], F32, name="bias32")
         biasT = const.tile([P, 2 * BLOCKS], F32, name="biasT")
         abT = const.tile([P, BLOCKS, P], F32, name="abT")
+        st = const.tile([P, BLOCKS, P], F32, name="st")
+        sel = const.tile([P, P], F32, name="sel")
 
         def small_inputs_cast():
-            nc.scalar.copy(out=ab32[:], in_=ab_bf[:])
-            nc.scalar.copy(out=bias32[:], in_=bias_bf[:])
+            nc.vector.tensor_copy(out=ab32[:], in_=ab_bf[:])
+            nc.vector.tensor_copy(out=bias32[:], in_=bias_bf[:])
 
         def small_inputs_transpose():
             ps_ab = bank("ps_ab")
@@ -114,6 +111,9 @@ def tile_bipartiteneuralmessagepassinglayer_pa_t_kernel(
                 nc.vector.tensor_scalar_add(
                     out=abT[:, m, NA:P], in0=ps_ab[:, m * P + NA : (m + 1) * P], scalar1=biasT[:, m : m + 1]
                 )
+            nc.vector.memset(st[:], 0.0)
+            nc.vector.tensor_tensor(out=sel[:, 0:NB], in0=ident[:, 0:NB], in1=ident[:, NB:P], op=ADD)
+            nc.vector.tensor_tensor(out=sel[:, NB:P], in0=ident[:, 0:NB], in1=ident[:, NB:P], op=ADD)
 
         wg = const.tile([P, PASSES, ED, PACK], BF16, name="wg", align_bytes=64)
         wq = const.tile([P, PASSES * ED], U32, name="wq", align_bytes=64)
@@ -302,36 +302,33 @@ def tile_bipartiteneuralmessagepassinglayer_pa_t_kernel(
                         stop=(c == NC - 1 and tl == TILES[c] - 1 and m == BLOCKS - 1),
                     )
 
-        small_inputs_cast()
         prep_we()
         transpose_x(0)
+        small_inputs_cast()
         ps_small = small_inputs_transpose()
         quant_x(0)
         small_inputs_finish(ps_small[0], ps_small[1])
         for k in range(NC + 2):
             if live(k - 1):
                 relu_regroup(k - 1)
-            if live(k + 1):
-                transpose_x(k + 1)
             if live(k - ACC_LAG):
                 accumulate(k - ACC_LAG)
             if k == NC + 1:
                 for c in range(k - ACC_LAG + 1, NC):
                     accumulate(c)
+            if live(k + 1):
+                transpose_x(k + 1)
             if live(k - 2):
                 sum_a(k - 2, 0, 2)
             if live(k - 1):
                 quant_h(k - 1)
+            if live(k - 2):
+                back(k - 2)
             if k == 0:
                 prep_we2_regroup()
             if live(k):
-                stage1(k, 0)
-                stage1(k, 1)
-            if live(k - 2):
-                back(k - 2)
-            if live(k):
-                stage1(k, 2)
-                stage1(k, 3)
+                for m in range(BLOCKS):
+                    stage1(k, m)
             if live(k + 1):
                 quant_x(k + 1)
             if k == 0:

from contextlib import ExitStack

import concourse.mybir as mybir
from concourse.masks import make_identity

F32 = mybir.dt.float32
BF16 = mybir.dt.bfloat16
U32 = mybir.dt.uint32
U8 = mybir.dt.uint8
FP8X4 = mybir.dt.float8_e4m3fn_x4
ADD = mybir.AluOpType.add
AX_X = mybir.AxisListType.X
RELU = mybir.ActivationFunctionType.Relu

P = 128
NA = 64
NB = 64
K1 = 1024
ED = 512
BLOCKS = ED // P
PACK = 4
PASSES = K1 // (P * PACK)
BANK = 512
PAIR = 2 * P
FLOPS = 2 * NA * NB * K1 * ED + 2 * NA * NB * ED * ED

TILES = (2, 2, 4, 4, 4, 4, 4, 4, 2, 2)
VECTOR_SUM_BLOCKS = 3
ACC_LAG = 3


def tile_bipartiteneuralmessagepassinglayer_pa_t_kernel(
    tc, edge_embeds, a_proj, b_proj, We, be1, We2, be2, out_0, out_1, out_2
):
    nc = tc.nc
    x_rows = edge_embeds.rearrange("i j k -> (i j) k")
    o_rows = out_0.rearrange("i j f -> (i j) f")
    NC = len(TILES)
    first_tile = [sum(TILES[:c]) for c in range(NC)]
    assert sum(TILES) * P == NA * NB

    with ExitStack() as ctx:
        const = ctx.enter_context(tc.tile_pool(name="const", bufs=1))
        work = ctx.enter_context(tc.tile_pool(name="work", bufs=2))
        psum = ctx.enter_context(tc.psum_pool(name="psum", bufs=7))
        psacc = ctx.enter_context(tc.psum_pool(name="psacc", bufs=1))
        ctx.enter_context(tc.manual_schedule())

        def bank(label):
            return psum.tile([P, BANK], F32, tag="bank", name=label)

        ab_bf = const.tile([P, ED], BF16, name="ab_bf")
        bias_bf = const.tile([P, P], BF16, name="bias_bf")
        nc.vector.memset(bias_bf[:], 0.0)
        nc.scalar.dma_start(out=ab_bf[0:NA, :], in_=a_proj)
        nc.scalar.dma_start(out=ab_bf[NA:P, :], in_=b_proj)
        nc.scalar.dma_start(out=bias_bf[0:BLOCKS, :], in_=be1.rearrange("(m f) -> m f", m=BLOCKS))
        nc.scalar.dma_start(out=bias_bf[BLOCKS : 2 * BLOCKS, :], in_=be2.rearrange("(m f) -> m f", m=BLOCKS))
        ident = const.tile([P, P], F32, name="ident")
        make_identity(nc, ident[:])
        acc = psacc.tile([P, ED], F32, name="acc")

        xs = []
        for c in range(NC):
            xs.append(const.tile([P, TILES[c], K1], BF16, name="x%d" % c))
        wraw = const.tile([P, 2 * PASSES, 2 * ED], BF16, name="wraw")
        w2raw = const.tile([P, PACK, ED], BF16, name="w2raw")
        we_view = We.rearrange("(gu p v) c -> p gu (v c)", gu=2 * PASSES, p=P, v=2)

        def load_x(c):
            r0 = first_tile[c] * P
            rows = x_rows[r0 : r0 + TILES[c] * P, :]
            nc.sync.dma_start(out=xs[c][:], in_=rows.rearrange("(t p) k -> p t k", p=P))

        def load_w(g):
            nc.sync.dma_start(out=wraw[:, 2 * g : 2 * g + 2, :], in_=we_view[:, 2 * g : 2 * g + 2, :])

        load_w(0)
        load_w(1)
        load_x(0)
        load_x(1)
        nc.sync.dma_start(out=w2raw[:], in_=We2.rearrange("(t p) c -> p t c", p=P))
        for c in range(2, NC):
            load_x(c)

        ab32 = const.tile([P, ED], F32, name="ab32")
        bias32 = const.tile([P, P], F32, name="bias32")
        biasT = const.tile([P, 2 * BLOCKS], F32, name="biasT")
        abT = const.tile([P, BLOCKS, P], F32, name="abT")
        st = const.tile([P, BLOCKS, P], F32, name="st")
        sel = const.tile([P, P], F32, name="sel")

        def small_inputs_cast():
            nc.vector.tensor_copy(out=ab32[:], in_=ab_bf[:])
            nc.vector.tensor_copy(out=bias32[:], in_=bias_bf[:])

        def small_inputs_transpose():
            ps_ab = bank("ps_ab")
            for m in range(BLOCKS):
                nc.tensor.transpose(ps_ab[:, m * P : (m + 1) * P], ab32[:, m * P : (m + 1) * P], ident[:])
            ps_bias = bank("ps_bias")
            nc.tensor.transpose(ps_bias[:, 0:P], bias32[:], ident[:])
            return ps_ab, ps_bias

        def small_inputs_finish(ps_ab, ps_bias):
            nc.vector.tensor_copy(out=biasT[:], in_=ps_bias[:, 0 : 2 * BLOCKS])
            nc.vector.tensor_copy(
                out=abT[:, :, 0:NA], in_=ps_ab[:].rearrange("p (m r) -> p m r", m=BLOCKS)[:, :, 0:NA]
            )
            for m in range(BLOCKS):
                nc.vector.tensor_scalar_add(
                    out=abT[:, m, NA:P], in0=ps_ab[:, m * P + NA : (m + 1) * P], scalar1=biasT[:, m : m + 1]
                )
            nc.vector.memset(st[:], 0.0)
            nc.vector.tensor_tensor(out=sel[:, 0:NB], in0=ident[:, 0:NB], in1=ident[:, NB:P], op=ADD)
            nc.vector.tensor_tensor(out=sel[:, NB:P], in0=ident[:, 0:NB], in1=ident[:, NB:P], op=ADD)

        wg = const.tile([P, PASSES, ED, PACK], BF16, name="wg", align_bytes=64)
        wq = const.tile([P, PASSES * ED], U32, name="wq", align_bytes=64)
        wsc = const.tile([P, PASSES * ED], U8, name="wsc", align_bytes=64)
        w2g = const.tile([P, ED, PACK], BF16, name="w2g", align_bytes=64)
        w2q = const.tile([P, ED], U32, name="w2q", align_bytes=64)
        w2sc = const.tile([P, ED], U8, name="w2sc", align_bytes=64)

        def regroup(eng_copy, dst, src):
            eng_copy(
                out=dst.rearrange("p (c z) t -> p c t z", z=4),
                in_=src.rearrange("p t (c z) -> p c t z", z=4),
            )

        def prep_we():
            for g in range(PASSES):
                src = wraw[:, 2 * g : 2 * g + 2, :].rearrange("p u (v c) -> p (u v) c", v=2)
                regroup(nc.vector.tensor_copy, wg[:, g, :, :], src)
            nc.vector.quantize_mx(
                out=wq[:].bitcast(FP8X4),
                scales=wsc[:],
                in_=wg[:].rearrange("p g c t -> p (g c t)"),
            )

        def prep_we2_regroup():
            regroup(nc.scalar.copy, w2g[:], w2raw[:])

        def prep_we2_quant():
            nc.vector.quantize_mx(
                out=w2q[:].bitcast(FP8X4), scales=w2sc[:], in_=w2g[:].rearrange("p c t -> p (c t)")
            )

        xg = {}
        xq = {}
        xsc = {}
        yy = {}
        hg = {}
        hq = {}
        hsc = {}
        lt = {}
        lo = {}

        def live(c):
            return 0 <= c < NC

        def transpose_x(c):
            n = TILES[c] * P
            xg[c] = work.tile([P, PASSES, n, 2], F32, name="xg%d" % c, tag="xg", align_bytes=64)
            for pair in range(TILES[c] // 2):
                for g in range(PASSES):
                    pb = bank("xt%d_%d_%d" % (c, g, pair))
                    for u in range(2):
                        for side in range(2):
                            words = xs[c][:, 2 * pair + side, :].bitcast(F32)
                            nc.tensor.transpose(
                                pb[:, u * PAIR + side * P : u * PAIR + (side + 1) * P],
                                words[:, 2 * P * g + P * u : 2 * P * g + P * (u + 1)],
                                ident[:],
                            )
                    nc.scalar.copy(
                        out=xg[c][:, g, pair * PAIR : (pair + 1) * PAIR, :],
                        in_=pb[:].rearrange("p (u e) -> p e u", u=2),
                    )

        def quant_x(c):
            n = TILES[c] * P
            xq[c] = work.tile([P, PASSES * n], U32, name="xq%d" % c, tag="xq", align_bytes=64)
            xsc[c] = work.tile([P, PASSES * n], U8, name="xsc%d" % c, tag="xsc", align_bytes=64)
            nc.vector.quantize_mx(
                out=xq[c][:].bitcast(FP8X4),
                scales=xsc[c][:],
                in_=xg[c][:].rearrange("p g e u -> p (g e u)").bitcast(BF16),
            )

        def stage1(c, m):
            n = TILES[c] * P
            if m == 0:
                yy[c] = work.tile([P, BLOCKS, n], BF16, name="y%d" % c, tag="y")
            pb = bank("p1_%d_%d" % (c, m))
            for g in range(PASSES):
                cols = slice(g * ED + m * P, g * ED + (m + 1) * P)
                nc.tensor.matmul_mx(
                    out=pb[:, 0:n],
                    lhsT=wq[:, cols].bitcast(FP8X4),
                    lhsT_scale=wsc[:, cols],
                    rhs=xq[c][:, g * n : (g + 1) * n].bitcast(FP8X4),
                    rhs_scale=xsc[c][:, g * n : (g + 1) * n],
                    start=(g == 0),
                    stop=(g == PASSES - 1),
                )
            for il in range(2 * TILES[c]):
                i = 2 * first_tile[c] + il
                nc.vector.scalar_tensor_tensor(
                    out=yy[c][:, m, il * NB : (il + 1) * NB],
                    in0=pb[:, il * NB : (il + 1) * NB],
                    scalar=abT[:, m, i : i + 1],
                    in1=abT[:, m, NA:P],
                    op0=ADD,
                    op1=ADD,
                )

        def relu_regroup(c):
            n = TILES[c] * P
            hg[c] = work.tile([P, n, PACK], BF16, name="hg%d" % c, tag="hg", align_bytes=64)
            nc.vector.tensor_scalar_max(
                out=hg[c][:].rearrange("p (c z) t -> p c t z", z=4),
                in0=yy[c][:].rearrange("p t (c z) -> p c t z", z=4),
                scalar1=0.0,
            )

        def quant_h(c):
            n = TILES[c] * P
            hq[c] = work.tile([P, n], U32, name="hq%d" % c, tag="hq", align_bytes=64)
            hsc[c] = work.tile([P, n], U8, name="hsc%d" % c, tag="hsc", align_bytes=64)
            nc.vector.quantize_mx(
                out=hq[c][:].bitcast(FP8X4),
                scales=hsc[c][:],
                in_=hg[c][:].rearrange("p e t -> p (e t)"),
            )

        def stage2(c, m):
            n = TILES[c] * P
            if m == 0:
                lt[c] = work.tile([P, BLOCKS, n], F32, name="lt%d" % c, tag="lt", bufs=ACC_LAG)
            pb = bank("p2_%d_%d" % (c, m))
            cols = slice(m * P, (m + 1) * P)
            nc.tensor.matmul_mx(
                out=pb[:, 0:n],
                lhsT=w2q[:, cols].bitcast(FP8X4),
                lhsT_scale=w2sc[:, cols],
                rhs=hq[c][:].bitcast(FP8X4),
                rhs_scale=hsc[c][:],
                start=True,
                stop=True,
            )
            if m < VECTOR_SUM_BLOCKS:
                nc.scalar.activation(
                    out=lt[c][:, m, :], in_=pb[:, 0:n], func=RELU, bias=biasT[:, BLOCKS + m : BLOCKS + m + 1], scale=1.0
                )
            else:
                for il in range(2 * TILES[c]):
                    i = 2 * first_tile[c] + il
                    nc.scalar.activation(
                        out=lt[c][:, m, il * NB : (il + 1) * NB],
                        in_=pb[:, il * NB : (il + 1) * NB],
                        func=RELU,
                        bias=biasT[:, BLOCKS + m : BLOCKS + m + 1],
                        scale=1.0,
                        accum_out=st[:, m, i : i + 1],
                    )

        def sum_a(c, m0, m1):
            i0 = 2 * first_tile[c]
            nc.vector.tensor_reduce(
                out=st[:, m0:m1, i0 : i0 + 2 * TILES[c]],
                in_=lt[c][:, m0:m1, :].rearrange("p m (i j) -> p m i j", j=NB),
                axis=AX_X,
                op=ADD,
            )

        def back(c):
            lo[c] = work.tile([P, TILES[c], ED], F32, name="lo%d" % c, tag="lo")
            r0 = first_tile[c] * P
            for tl in range(TILES[c]):
                pb = bank("lb%d_%d" % (c, tl))
                for m in range(BLOCKS):
                    nc.tensor.transpose(
                        pb[:, m * P : (m + 1) * P], lt[c][:, m, tl * P : (tl + 1) * P], ident[:]
                    )
                nc.scalar.copy(out=lo[c][:, tl, :], in_=pb[:])
                if c == NC - 1:
                    nc.sync.dma_start(out=o_rows[r0 + tl * P : r0 + (tl + 1) * P, :], in_=lo[c][:, tl, :])
            if c < NC - 1:
                rows = o_rows[r0 : r0 + TILES[c] * P, :]
                nc.sync.dma_start(out=rows.rearrange("(t p) f -> p t f", p=P), in_=lo[c][:])

        def accumulate(c):
            for tl in range(TILES[c]):
                for m in range(BLOCKS):
                    nc.tensor.matmul(
                        out=acc[:, m * P : (m + 1) * P],
                        lhsT=lt[c][:, m, tl * P : (tl + 1) * P],
                        rhs=ident[:],
                        is_transpose=True,
                        start=(c == 0 and tl == 0 and m == 0),
                        stop=(c == NC - 1 and tl == TILES[c] - 1 and m == BLOCKS - 1),
                    )

        prep_we()
        transpose_x(0)
        small_inputs_cast()
        ps_small = small_inputs_transpose()
        quant_x(0)
        small_inputs_finish(ps_small[0], ps_small[1])
        for k in range(NC + 2):
            if live(k - 1):
                relu_regroup(k - 1)
            if live(k - ACC_LAG):
                accumulate(k - ACC_LAG)
            if k == NC + 1:
                for c in range(k - ACC_LAG + 1, NC):
                    accumulate(c)
            if live(k + 1):
                transpose_x(k + 1)
            if live(k - 2):
                sum_a(k - 2, 0, 2)
            if live(k - 1):
                quant_h(k - 1)
            if live(k - 2):
                back(k - 2)
            if k == 0:
                prep_we2_regroup()
            if live(k):
                for m in range(BLOCKS):
                    stage1(k, m)
            if live(k + 1):
                quant_x(k + 1)
            if k == 0:
                prep_we2_quant()
            if live(k - 1):
                for m in range(BLOCKS):
                    stage2(k - 1, m)
            if live(k - 2):
                sum_a(k - 2, 2, VECTOR_SUM_BLOCKS)

        pa = bank("ps_suma")
        for m in range(BLOCKS):
            nc.tensor.transpose(pa[:, m * P : (m + 1) * P], st[:, m, :], ident[:])
        so_a = const.tile([P, ED], F32, name="so_a")
        nc.scalar.copy(out=so_a[:], in_=pa[:])
        nc.sync.dma_start(out=out_1, in_=so_a[0:NA, :])
        acc_sb = const.tile([P, ED], F32, name="acc_sb")
        nc.vector.tensor_copy(out=acc_sb[:], in_=acc[:])
        pb = bank("ps_sumb")
        nc.tensor.matmul(out=pb[:], lhsT=sel[:], rhs=acc_sb[:], start=True, stop=True)
        so_b = const.tile([P, ED], F32, name="so_b")
        nc.vector.tensor_copy(out=so_b[:], in_=pb[:])
        nc.sync.dma_start(out=out_2, in_=so_b[0:NB, :])
